import numpy as np
import ml_dtypes


def mxq(x, axis, fmt="e4m3"):
    dtype, down = {"e4m3": (ml_dtypes.float8_e4m3fn, 7), "e5m2": (ml_dtypes.float8_e5m2, 14)}[fmt]
    v = np.moveaxis(np.asarray(x, np.float32).astype(ml_dtypes.bfloat16).astype(np.float64), axis, -1)
    blocks = v.reshape(v.shape[:-1] + (-1, 32))
    amax = np.abs(blocks).max(-1, keepdims=True)
    byte = np.maximum(np.where(amax > 0, np.frexp(amax)[1] - 1 + 127, 0) - down, 1)
    scale = np.exp2(byte - 127.0)
    codes = (blocks / scale).astype(np.float32).astype(dtype).astype(np.float64)
    return np.moveaxis((codes * scale).reshape(v.shape), -1, axis)


WIDE = False


def mx_kscale(k):
    if not WIDE:
        return np.ones(k)
    levels = np.array([10, -10, 5, -5, 0])
    a = np.random.permutation(np.resize(levels, k // 512 * 4)).reshape(k // 512, 4)
    idx = np.arange(k)
    return np.exp2(a[idx // 512, idx % 128 // 32])


BF16 = ml_dtypes.bfloat16


def bf(x):
    return np.asarray(x, np.float32).astype(BF16)


def f64(x):
    return np.asarray(x).astype(np.float64)


B, S, SV, H, DH = 1, 1024, 1024, 8, 64
SCALE = DH ** (-0.5)


def _flatten_like_module(t):
    b, s, h, dh = t.shape
    return np.transpose(t, (0, 2, 1, 3)).reshape(b, s, h * dh)


def _heads_to_batch(t):
    b, s, d = t.shape
    t = t.reshape(b, s, H, d // H)
    t = np.transpose(t, (0, 2, 1, 3))
    return t.reshape(b * H, s, d // H)


def setup_inputs():
    a = np.sqrt(2.0 / (SCALE * np.sqrt(S)))
    sc = mx_kscale(S)
    f = np.repeat(sc.reshape(H, S // H).T, H, axis=0)[None, :, :, None]
    return {"query": bf(np.random.standard_normal((B, S, H, DH)) * a * f),
            "key": bf(np.random.standard_normal((B, S, H, DH)) * a / f),
            "value": bf(np.random.standard_normal((B, SV, H, DH)))}


def reference(query, key, value):
    q = _heads_to_batch(_flatten_like_module(f64(query)))
    k = _heads_to_batch(_flatten_like_module(f64(key)))
    scores = (mxq(q, 1, "e4m3").transpose(0, 2, 1) @ mxq(k, 1, "e4m3")) * SCALE
    e = np.exp(scores - scores.max(axis=2, keepdims=True))
    return e / e.sum(axis=2, keepdims=True)

@@ -1,0 +1,125 @@
+from contextlib import ExitStack
+
+import concourse.mybir as mybir
+
+BF16 = mybir.dt.bfloat16
+F32 = mybir.dt.float32
+U32 = mybir.dt.uint32
+U8 = mybir.dt.uint8
+FP8X4 = mybir.dt.float8_e4m3fn_x4
+ALU = mybir.AluOpType
+ACT = mybir.ActivationFunctionType
+AXIS = mybir.AxisListType
+
+P = 128
+PACK = 4
+SEQ, HEADS, DH = 1024, 8, 64
+MATS = SEQ // P
+PASSES = HEADS // PACK
+DUO = 2
+PAIRS = MATS // DUO
+COLS = DUO * DH
+RUN = 4
+SCALE = DH ** -0.5
+
+FLOPS = 2 * MATS * DH * DH * SEQ
+BYTES = 2 * SEQ * HEADS * DH * 2 + MATS * DH * DH * 4
+
+
+def regroup(copy, raw, grouped):
+    for c in range(PASSES):
+        copy(
+            out=grouped[:, c].rearrange("p a (e i) t -> p a e t i", i=RUN),
+            in_=raw[:, :, c].rearrange("p a t (e i) -> p a e t i", i=RUN),
+        )
+
+
+def tile_flaxattention2_s_kernel(tc, query, key, value, out):
+    nc = tc.nc
+    q_view = query.rearrange("b (j g) (c t) d -> (b j) g c t d", g=MATS, t=PACK)
+    k_view = key.rearrange("b (j g) (c t) d -> (b j) g c t d", g=MATS, t=PACK)
+    out_view = out.rearrange("(pair a) d e -> (a d) pair e", a=DUO)
+
+    with ExitStack() as ctx:
+        loads = ctx.enter_context(tc.tile_pool(name="loads", bufs=PAIRS))
+        operands = ctx.enter_context(tc.tile_pool(name="operands", bufs=PAIRS))
+        soft = ctx.enter_context(tc.tile_pool(name="soft", bufs=1))
+        psum = ctx.enter_context(tc.psum_pool(name="psum", bufs=1))
+
+        k_raw_tiles = []
+        q_raw_tiles = []
+        for pair in range(PAIRS):
+            mats = slice(pair * DUO, (pair + 1) * DUO)
+            k_raw = loads.tile([P, DUO, PASSES, PACK, DH], BF16)
+            nc.sync.dma_start(out=k_raw[:], in_=k_view[:, mats])
+            k_raw_tiles.append(k_raw)
+            q_raw = loads.tile([P, DUO, PASSES, PACK, DH], BF16)
+            nc.sync.dma_start(out=q_raw[:], in_=q_view[:, mats])
+            q_raw_tiles.append(q_raw)
+
+        warm = soft.tile([P, 1], F32)
+        nc.vector.memset(warm[:], 0.0)
+        nc.scalar.activation(out=warm[:], in_=warm[:], func=ACT.Exp)
+
+        scores = psum.tile([P, PAIRS, COLS], F32)
+
+        for pair in range(PAIRS):
+            q_grouped = operands.tile([P, PASSES, DUO, DH, PACK], BF16, align_bytes=64)
+            k_grouped = operands.tile([P, PASSES, DUO, DH, PACK], BF16, align_bytes=64)
+            regroup(nc.vector.tensor_copy, q_raw_tiles[pair], q_grouped)
+            regroup(nc.scalar.copy, k_raw_tiles[pair], k_grouped)
+
+            q_codes = operands.tile([P, PASSES * COLS], U32, align_bytes=64)
+            q_scales = operands.tile([P, PASSES * COLS], U8, align_bytes=64)
+            k_codes = operands.tile([P, PASSES * COLS], U32, align_bytes=64)
+            k_scales = operands.tile([P, PASSES * COLS], U8, align_bytes=64)
+            nc.vector.quantize_mx(
+                out=q_codes[:].bitcast(FP8X4),
+                scales=q_scales[:],
+                in_=q_grouped[:].rearrange("p c a d t -> p (c a d t)"),
+            )
+            nc.vector.quantize_mx(
+                out=k_codes[:].bitcast(FP8X4),
+                scales=k_scales[:],
+                in_=k_grouped[:].rearrange("p c a d t -> p (c a d t)"),
+            )
+
+            for c in range(PASSES):
+                cols = slice(c * COLS, (c + 1) * COLS)
+                nc.tensor.matmul_mx(
+                    out=scores[:, pair, :],
+                    lhsT=q_codes[:, cols].bitcast(FP8X4),
+                    lhsT_scale=q_scales[:, cols],
+                    rhs=k_codes[:, cols].bitcast(FP8X4),
+                    rhs_scale=k_scales[:, cols],
+                    start=(c == 0),
+                    stop=(c == PASSES - 1),
+                )
+
+        row_max = soft.tile([P, PAIRS], F32)
+        shifted = soft.tile([P, PAIRS, DH], F32)
+        for a in range(DUO):
+            half = slice(a * DH, (a + 1) * DH)
+            nc.vector.reduce_max(out=row_max[half, :], in_=scores[half, :, half], axis=AXIS.X)
+        for a in range(DUO):
+            half = slice(a * DH, (a + 1) * DH)
+            nc.vector.tensor_tensor(
+                out=shifted[half],
+                in0=scores[half, :, half],
+                in1=row_max[half, :].unsqueeze(2).to_broadcast([DH, PAIRS, DH]),
+                op=ALU.subtract,
+            )
+        grown = soft.tile([P, PAIRS, DH], F32)
+        nc.scalar.activation(out=grown[:], in_=shifted[:], func=ACT.Exp, scale=SCALE)
+        row_sum = soft.tile([P, PAIRS], F32)
+        nc.vector.reduce_sum(out=row_sum[:], in_=grown[:], axis=AXIS.X)
+        inverse = soft.tile([P, PAIRS], F32)
+        nc.vector.reciprocal(out=inverse[:], in_=row_sum[:])
+        probs = soft.tile([P, PAIRS, DH], F32)
+        nc.vector.tensor_tensor(
+            out=probs[:],
+            in0=grown[:],
+            in1=inverse[:].unsqueeze(2).to_broadcast([P, PAIRS, DH]),
+            op=ALU.mult,
+        )
+        nc.sync.dma_start(out=out_view, in_=probs[:])

@@ -27,11 +27,10 @@ BYTES = 2 * SEQ * HEADS * DH * 2 + MATS * DH * DH * 4
 
 
 def regroup(copy, raw, grouped):
-    for c in range(PASSES):
-        copy(
-            out=grouped[:, c].rearrange("p a (e i) t -> p a e t i", i=RUN),
-            in_=raw[:, :, c].rearrange("p a t (e i) -> p a e t i", i=RUN),
-        )
+    copy(
+        out=grouped.rearrange("p a (e i) t -> p a e t i", i=RUN),
+        in_=raw.rearrange("p a t (e i) -> p a e t i", i=RUN),
+    )
 
 
 def tile_flaxattention2_s_kernel(tc, query, key, value, out):
@@ -42,9 +41,9 @@ def tile_flaxattention2_s_kernel(tc, query, key, value, out):
 
     with ExitStack() as ctx:
         loads = ctx.enter_context(tc.tile_pool(name="loads", bufs=PAIRS))
-        operands = ctx.enter_context(tc.tile_pool(name="operands", bufs=PAIRS))
+        operands = ctx.enter_context(tc.tile_pool(name="operands", bufs=PAIRS * PASSES))
         soft = ctx.enter_context(tc.tile_pool(name="soft", bufs=1))
-        psum = ctx.enter_context(tc.psum_pool(name="psum", bufs=1))
+        psum = ctx.enter_context(tc.psum_pool(name="psum", bufs=PAIRS))
 
         k_raw_tiles = []
         q_raw_tiles = []
@@ -61,65 +60,75 @@ def tile_flaxattention2_s_kernel(tc, query, key, value, out):
         nc.vector.memset(warm[:], 0.0)
         nc.scalar.activation(out=warm[:], in_=warm[:], func=ACT.Exp)
 
-        scores = psum.tile([P, PAIRS, COLS], F32)
-
+        score_tiles = []
         for pair in range(PAIRS):
-            q_grouped = operands.tile([P, PASSES, DUO, DH, PACK], BF16, align_bytes=64)
-            k_grouped = operands.tile([P, PASSES, DUO, DH, PACK], BF16, align_bytes=64)
-            regroup(nc.vector.tensor_copy, q_raw_tiles[pair], q_grouped)
-            regroup(nc.scalar.copy, k_raw_tiles[pair], k_grouped)
-
-            q_codes = operands.tile([P, PASSES * COLS], U32, align_bytes=64)
-            q_scales = operands.tile([P, PASSES * COLS], U8, align_bytes=64)
-            k_codes = operands.tile([P, PASSES * COLS], U32, align_bytes=64)
-            k_scales = operands.tile([P, PASSES * COLS], U8, align_bytes=64)
-            nc.vector.quantize_mx(
-                out=q_codes[:].bitcast(FP8X4),
-                scales=q_scales[:],
-                in_=q_grouped[:].rearrange("p c a d t -> p (c a d t)"),
-            )
-            nc.vector.quantize_mx(
-                out=k_codes[:].bitcast(FP8X4),
-                scales=k_scales[:],
-                in_=k_grouped[:].rearrange("p c a d t -> p (c a d t)"),
-            )
-
+            scores = psum.tile([P, COLS], F32)
+            score_tiles.append(scores)
             for c in range(PASSES):
-                cols = slice(c * COLS, (c + 1) * COLS)
+                k_grouped = operands.tile([P, DUO, DH, PACK], BF16, align_bytes=64)
+                q_grouped = operands.tile([P, DUO, DH, PACK], BF16, align_bytes=64)
+                regroup(nc.scalar.copy, k_raw_tiles[pair][:, :, c], k_grouped[:])
+                regroup(nc.vector.tensor_copy, q_raw_tiles[pair][:, :, c], q_grouped[:])
+
+                k_codes = operands.tile([P, COLS], U32, align_bytes=64)
+                k_scales = operands.tile([P, COLS], U8, align_bytes=64)
+                q_codes = operands.tile([P, COLS], U32, align_bytes=64)
+                q_scales = operands.tile([P, COLS], U8, align_bytes=64)
+                nc.vector.quantize_mx(
+                    out=k_codes[:].bitcast(FP8X4),
+                    scales=k_scales[:],
+                    in_=k_grouped[:].rearrange("p a d t -> p (a d t)"),
+                )
+                nc.vector.quantize_mx(
+                    out=q_codes[:].bitcast(FP8X4),
+                    scales=q_scales[:],
+                    in_=q_grouped[:].rearrange("p a d t -> p (a d t)"),
+                )
                 nc.tensor.matmul_mx(
-                    out=scores[:, pair, :],
-                    lhsT=q_codes[:, cols].bitcast(FP8X4),
-                    lhsT_scale=q_scales[:, cols],
-                    rhs=k_codes[:, cols].bitcast(FP8X4),
-                    rhs_scale=k_scales[:, cols],
+                    out=scores[:],
+                    lhsT=q_codes[:].bitcast(FP8X4),
+                    lhsT_scale=q_scales[:],
+                    rhs=k_codes[:].bitcast(FP8X4),
+                    rhs_scale=k_scales[:],
                     start=(c == 0),
                     stop=(c == PASSES - 1),
                 )
 
         row_max = soft.tile([P, PAIRS], F32)
-        shifted = soft.tile([P, PAIRS, DH], F32)
-        for a in range(DUO):
-            half = slice(a * DH, (a + 1) * DH)
-            nc.vector.reduce_max(out=row_max[half, :], in_=scores[half, :, half], axis=AXIS.X)
-        for a in range(DUO):
-            half = slice(a * DH, (a + 1) * DH)
-            nc.vector.tensor_tensor(
-                out=shifted[half],
-                in0=scores[half, :, half],
-                in1=row_max[half, :].unsqueeze(2).to_broadcast([DH, PAIRS, DH]),
-                op=ALU.subtract,
-            )
-        grown = soft.tile([P, PAIRS, DH], F32)
-        nc.scalar.activation(out=grown[:], in_=shifted[:], func=ACT.Exp, scale=SCALE)
+        shift = soft.tile([P, PAIRS], F32)
         row_sum = soft.tile([P, PAIRS], F32)
-        nc.vector.reduce_sum(out=row_sum[:], in_=grown[:], axis=AXIS.X)
         inverse = soft.tile([P, PAIRS], F32)
-        nc.vector.reciprocal(out=inverse[:], in_=row_sum[:])
+        grown = soft.tile([P, PAIRS, DH], F32)
         probs = soft.tile([P, PAIRS, DH], F32)
-        nc.vector.tensor_tensor(
-            out=probs[:],
-            in0=grown[:],
-            in1=inverse[:].unsqueeze(2).to_broadcast([P, PAIRS, DH]),
-            op=ALU.mult,
-        )
-        nc.sync.dma_start(out=out_view, in_=probs[:])
+
+        for pair in range(PAIRS):
+            scores = score_tiles[pair]
+            one = slice(pair, pair + 1)
+            for a in range(DUO):
+                half = slice(a * DH, (a + 1) * DH)
+                nc.vector.reduce_max(out=row_max[half, one], in_=scores[half, half], axis=AXIS.X)
+            nc.vector.tensor_scalar(
+                out=shift[:, one], in0=row_max[:, one], scalar1=-SCALE, scalar2=None, op0=ALU.mult
+            )
+            for a in range(DUO):
+                half = slice(a * DH, (a + 1) * DH)
+                nc.scalar.activation(
+                    out=grown[half, pair, :],
+                    in_=scores[half, half],
+                    func=ACT.Exp,
+                    bias=shift[half, one],
+                    scale=SCALE,
+                    accum_out=row_sum[half, one],
+                )
+
+        for pair in range(PAIRS):
+            one = slice(pair, pair + 1)
+            nc.vector.reciprocal(out=inverse[:, one], in_=row_sum[:, one])
+            nc.vector.tensor_scalar(
+                out=probs[:, pair, :],
+                in0=grown[:, pair, :],
+                scalar1=inverse[:, one],
+                scalar2=None,
+                op0=ALU.mult,
+            )
+            nc.sync.dma_start(out=out_view[:, pair, :], in_=probs[:, pair, :])

@@ -19,6 +19,7 @@ PASSES = HEADS // PACK
 DUO = 2
 PAIRS = MATS // DUO
 COLS = DUO * DH
+UNITS = PAIRS * PASSES
 RUN = 4
 SCALE = DH ** -0.5
 
@@ -40,8 +41,9 @@ def tile_flaxattention2_s_kernel(tc, query, key, value, out):
     out_view = out.rearrange("(pair a) d e -> (a d) pair e", a=DUO)
 
     with ExitStack() as ctx:
+        ctx.enter_context(tc.manual_schedule())
         loads = ctx.enter_context(tc.tile_pool(name="loads", bufs=PAIRS))
-        operands = ctx.enter_context(tc.tile_pool(name="operands", bufs=PAIRS * PASSES))
+        operands = ctx.enter_context(tc.tile_pool(name="operands", bufs=UNITS))
         soft = ctx.enter_context(tc.tile_pool(name="soft", bufs=1))
         psum = ctx.enter_context(tc.psum_pool(name="psum", bufs=PAIRS))
 
@@ -64,66 +66,93 @@ def tile_flaxattention2_s_kernel(tc, query, key, value, out):
         for pair in range(PAIRS):
             scores = psum.tile([P, COLS], F32)
             score_tiles.append(scores)
-            for c in range(PASSES):
-                k_grouped = operands.tile([P, DUO, DH, PACK], BF16, align_bytes=64)
-                q_grouped = operands.tile([P, DUO, DH, PACK], BF16, align_bytes=64)
-                regroup(nc.scalar.copy, k_raw_tiles[pair][:, :, c], k_grouped[:])
-                regroup(nc.vector.tensor_copy, q_raw_tiles[pair][:, :, c], q_grouped[:])
 
-                k_codes = operands.tile([P, COLS], U32, align_bytes=64)
-                k_scales = operands.tile([P, COLS], U8, align_bytes=64)
-                q_codes = operands.tile([P, COLS], U32, align_bytes=64)
-                q_scales = operands.tile([P, COLS], U8, align_bytes=64)
-                nc.vector.quantize_mx(
-                    out=k_codes[:].bitcast(FP8X4),
-                    scales=k_scales[:],
-                    in_=k_grouped[:].rearrange("p a d t -> p (a d t)"),
-                )
-                nc.vector.quantize_mx(
-                    out=q_codes[:].bitcast(FP8X4),
-                    scales=q_scales[:],
-                    in_=q_grouped[:].rearrange("p a d t -> p (a d t)"),
-                )
-                nc.tensor.matmul_mx(
-                    out=scores[:],
-                    lhsT=q_codes[:].bitcast(FP8X4),
-                    lhsT_scale=q_scales[:],
-                    rhs=k_codes[:].bitcast(FP8X4),
-                    rhs_scale=k_scales[:],
-                    start=(c == 0),
-                    stop=(c == PASSES - 1),
-                )
+        k_grouped_tiles = []
+        q_grouped_tiles = []
+        k_code_tiles = []
+        k_scale_tiles = []
 
-        row_max = soft.tile([P, PAIRS], F32)
+        def regroup_unit(unit):
+            pair, c = divmod(unit, PASSES)
+            k_grouped = operands.tile([P, DUO, DH, PACK], BF16, align_bytes=64)
+            regroup(nc.scalar.copy, k_raw_tiles[pair][:, :, c], k_grouped[:])
+            k_grouped_tiles.append(k_grouped)
+            q_grouped = operands.tile([P, DUO, DH, PACK], BF16, align_bytes=64)
+            regroup(nc.vector.tensor_copy, q_raw_tiles[pair][:, :, c], q_grouped[:])
+            q_grouped_tiles.append(q_grouped)
+
+        def quantise_k(unit):
+            k_codes = operands.tile([P, COLS], U32, align_bytes=64)
+            k_scales = operands.tile([P, COLS], U8, align_bytes=64)
+            nc.vector.quantize_mx(
+                out=k_codes[:].bitcast(FP8X4),
+                scales=k_scales[:],
+                in_=k_grouped_tiles[unit][:].rearrange("p a d t -> p (a d t)"),
+            )
+            k_code_tiles.append(k_codes)
+            k_scale_tiles.append(k_scales)
+
+        def quantise_q_and_multiply(unit):
+            pair, c = divmod(unit, PASSES)
+            q_codes = operands.tile([P, COLS], U32, align_bytes=64)
+            q_scales = operands.tile([P, COLS], U8, align_bytes=64)
+            nc.vector.quantize_mx(
+                out=q_codes[:].bitcast(FP8X4),
+                scales=q_scales[:],
+                in_=q_grouped_tiles[unit][:].rearrange("p a d t -> p (a d t)"),
+            )
+            nc.tensor.matmul_mx(
+                out=score_tiles[pair][:],
+                lhsT=q_codes[:].bitcast(FP8X4),
+                lhsT_scale=q_scales[:],
+                rhs=k_code_tiles[unit][:].bitcast(FP8X4),
+                rhs_scale=k_scale_tiles[unit][:],
+                start=(c == 0),
+                stop=(c == PASSES - 1),
+            )
+
+        regroup_unit(0)
+        quantise_k(0)
+        for unit in range(1, UNITS):
+            regroup_unit(unit)
+            quantise_q_and_multiply(unit - 1)
+            quantise_k(unit)
+        quantise_q_and_multiply(UNITS - 1)
+
+        flipped = soft.tile([P, PAIRS, DH], F32)
         shift = soft.tile([P, PAIRS], F32)
+        grown = soft.tile([P, PAIRS, DH], F32)
         row_sum = soft.tile([P, PAIRS], F32)
         inverse = soft.tile([P, PAIRS], F32)
-        grown = soft.tile([P, PAIRS, DH], F32)
         probs = soft.tile([P, PAIRS, DH], F32)
 
         for pair in range(PAIRS):
-            scores = score_tiles[pair]
             one = slice(pair, pair + 1)
             for a in range(DUO):
                 half = slice(a * DH, (a + 1) * DH)
-                nc.vector.reduce_max(out=row_max[half, one], in_=scores[half, half], axis=AXIS.X)
-            nc.vector.tensor_scalar(
-                out=shift[:, one], in0=row_max[:, one], scalar1=-SCALE, scalar2=None, op0=ALU.mult
-            )
-            for a in range(DUO):
-                half = slice(a * DH, (a + 1) * DH)
-                nc.scalar.activation(
-                    out=grown[half, pair, :],
-                    in_=scores[half, half],
-                    func=ACT.Exp,
-                    bias=shift[half, one],
-                    scale=SCALE,
-                    accum_out=row_sum[half, one],
+                nc.vector.tensor_scalar(
+                    out=flipped[half, pair, :],
+                    in0=score_tiles[pair][half, half],
+                    scalar1=-SCALE,
+                    scalar2=None,
+                    op0=ALU.mult,
+                    op1=ALU.min,
+                    accum_out=shift[half, one],
                 )
+            nc.scalar.activation(
+                out=grown[:, pair, :],
+                in_=flipped[:, pair, :],
+                func=ACT.Exp,
+                bias=shift[:, one],
+                scale=-1.0,
+                accum_out=row_sum[:, one],
+            )
 
         for pair in range(PAIRS):
             one = slice(pair, pair + 1)
             nc.vector.reciprocal(out=inverse[:, one], in_=row_sum[:, one])
+        for pair in range(PAIRS):
+            one = slice(pair, pair + 1)
             nc.vector.tensor_scalar(
                 out=probs[:, pair, :],
                 in0=grown[:, pair, :],

@@ -9,7 +9,6 @@ U8 = mybir.dt.uint8
 FP8X4 = mybir.dt.float8_e4m3fn_x4
 ALU = mybir.AluOpType
 ACT = mybir.ActivationFunctionType
-AXIS = mybir.AxisListType
 
 P = 128
 PACK = 4
@@ -19,7 +18,6 @@ PASSES = HEADS // PACK
 DUO = 2
 PAIRS = MATS // DUO
 COLS = DUO * DH
-UNITS = PAIRS * PASSES
 RUN = 4
 SCALE = DH ** -0.5
 
@@ -43,7 +41,7 @@ def tile_flaxattention2_s_kernel(tc, query, key, value, out):
     with ExitStack() as ctx:
         ctx.enter_context(tc.manual_schedule())
         loads = ctx.enter_context(tc.tile_pool(name="loads", bufs=PAIRS))
-        operands = ctx.enter_context(tc.tile_pool(name="operands", bufs=UNITS))
+        operands = ctx.enter_context(tc.tile_pool(name="operands", bufs=PAIRS))
         soft = ctx.enter_context(tc.tile_pool(name="soft", bufs=1))
         psum = ctx.enter_context(tc.psum_pool(name="psum", bufs=PAIRS))
 
@@ -62,62 +60,65 @@ def tile_flaxattention2_s_kernel(tc, query, key, value, out):
         nc.vector.memset(warm[:], 0.0)
         nc.scalar.activation(out=warm[:], in_=warm[:], func=ACT.Exp)
 
-        score_tiles = []
-        for pair in range(PAIRS):
-            scores = psum.tile([P, COLS], F32)
-            score_tiles.append(scores)
+        def regroup_both_passes(raw, grouped):
+            regroup(nc.scalar.copy, raw[:, :, 0], grouped[:, 0])
+            regroup(nc.vector.tensor_copy, raw[:, :, 1], grouped[:, 1])
+
+        def quantise(grouped, codes, scales):
+            nc.vector.quantize_mx(
+                out=codes[:].bitcast(FP8X4),
+                scales=scales[:],
+                in_=grouped[:].rearrange("p c a d t -> p (c a d t)"),
+            )
 
         k_grouped_tiles = []
         q_grouped_tiles = []
         k_code_tiles = []
         k_scale_tiles = []
+        score_tiles = []
 
-        def regroup_unit(unit):
-            pair, c = divmod(unit, PASSES)
-            k_grouped = operands.tile([P, DUO, DH, PACK], BF16, align_bytes=64)
-            regroup(nc.scalar.copy, k_raw_tiles[pair][:, :, c], k_grouped[:])
+        def regroup_k(pair):
+            k_grouped = operands.tile([P, PASSES, DUO, DH, PACK], BF16, align_bytes=64)
+            regroup_both_passes(k_raw_tiles[pair], k_grouped)
             k_grouped_tiles.append(k_grouped)
-            q_grouped = operands.tile([P, DUO, DH, PACK], BF16, align_bytes=64)
-            regroup(nc.vector.tensor_copy, q_raw_tiles[pair][:, :, c], q_grouped[:])
+
+        def regroup_q(pair):
+            q_grouped = operands.tile([P, PASSES, DUO, DH, PACK], BF16, align_bytes=64)
+            regroup_both_passes(q_raw_tiles[pair], q_grouped)
             q_grouped_tiles.append(q_grouped)
 
-        def quantise_k(unit):
-            k_codes = operands.tile([P, COLS], U32, align_bytes=64)
-            k_scales = operands.tile([P, COLS], U8, align_bytes=64)
-            nc.vector.quantize_mx(
-                out=k_codes[:].bitcast(FP8X4),
-                scales=k_scales[:],
-                in_=k_grouped_tiles[unit][:].rearrange("p a d t -> p (a d t)"),
-            )
+        def quantise_k(pair):
+            k_codes = operands.tile([P, PASSES * COLS], U32, align_bytes=64)
+            k_scales = operands.tile([P, PASSES * COLS], U8, align_bytes=64)
+            quantise(k_grouped_tiles[pair], k_codes, k_scales)
             k_code_tiles.append(k_codes)
             k_scale_tiles.append(k_scales)
 
-        def quantise_q_and_multiply(unit):
-            pair, c = divmod(unit, PASSES)
-            q_codes = operands.tile([P, COLS], U32, align_bytes=64)
-            q_scales = operands.tile([P, COLS], U8, align_bytes=64)
-            nc.vector.quantize_mx(
-                out=q_codes[:].bitcast(FP8X4),
-                scales=q_scales[:],
-                in_=q_grouped_tiles[unit][:].rearrange("p a d t -> p (a d t)"),
-            )
-            nc.tensor.matmul_mx(
-                out=score_tiles[pair][:],
-                lhsT=q_codes[:].bitcast(FP8X4),
-                lhsT_scale=q_scales[:],
-                rhs=k_code_tiles[unit][:].bitcast(FP8X4),
-                rhs_scale=k_scale_tiles[unit][:],
-                start=(c == 0),
-                stop=(c == PASSES - 1),
-            )
+        def quantise_q_and_multiply(pair):
+            q_codes = operands.tile([P, PASSES * COLS], U32, align_bytes=64)
+            q_scales = operands.tile([P, PASSES * COLS], U8, align_bytes=64)
+            quantise(q_grouped_tiles[pair], q_codes, q_scales)
+            scores = psum.tile([P, COLS], F32)
+            score_tiles.append(scores)
+            for c in range(PASSES):
+                cols = slice(c * COLS, (c + 1) * COLS)
+                nc.tensor.matmul_mx(
+                    out=scores[:],
+                    lhsT=q_codes[:, cols].bitcast(FP8X4),
+                    lhsT_scale=q_scales[:, cols],
+                    rhs=k_code_tiles[pair][:, cols].bitcast(FP8X4),
+                    rhs_scale=k_scale_tiles[pair][:, cols],
+                    start=(c == 0),
+                    stop=(c == PASSES - 1),
+                )
 
-        regroup_unit(0)
-        quantise_k(0)
-        for unit in range(1, UNITS):
-            regroup_unit(unit)
-            quantise_q_and_multiply(unit - 1)
-            quantise_k(unit)
-        quantise_q_and_multiply(UNITS - 1)
+        for pair in range(PAIRS):
+            regroup_k(pair)
+            if pair > 0:
+                quantise_q_and_multiply(pair - 1)
+            regroup_q(pair)
+            quantise_k(pair)
+        quantise_q_and_multiply(PAIRS - 1)
 
         flipped = soft.tile([P, PAIRS, DH], F32)
         shift = soft.tile([P, PAIRS], F32)
@@ -148,16 +149,17 @@ def tile_flaxattention2_s_kernel(tc, query, key, value, out):
                 accum_out=row_sum[:, one],
             )
 
-        for pair in range(PAIRS):
-            one = slice(pair, pair + 1)
-            nc.vector.reciprocal(out=inverse[:, one], in_=row_sum[:, one])
-        for pair in range(PAIRS):
-            one = slice(pair, pair + 1)
-            nc.vector.tensor_scalar(
-                out=probs[:, pair, :],
-                in0=grown[:, pair, :],
-                scalar1=inverse[:, one],
-                scalar2=None,
-                op0=ALU.mult,
-            )
-            nc.sync.dma_start(out=out_view[:, pair, :], in_=probs[:, pair, :])
+        for group in (range(PAIRS - 1), range(PAIRS - 1, PAIRS)):
+            for pair in group:
+                one = slice(pair, pair + 1)
+                nc.vector.reciprocal(out=inverse[:, one], in_=row_sum[:, one])
+            for pair in group:
+                one = slice(pair, pair + 1)
+                nc.vector.tensor_scalar(
+                    out=probs[:, pair, :],
+                    in0=grown[:, pair, :],
+                    scalar1=inverse[:, one],
+                    scalar2=None,
+                    op0=ALU.mult,
+                )
+                nc.sync.dma_start(out=out_view[:, pair, :], in_=probs[:, pair, :])

@@ -64,12 +64,6 @@ def tile_flaxattention2_s_kernel(tc, query, key, value, out):
             regroup(nc.scalar.copy, raw[:, :, 0], grouped[:, 0])
             regroup(nc.vector.tensor_copy, raw[:, :, 1], grouped[:, 1])
 
-        def quantise(grouped, codes, scales):
-            nc.vector.quantize_mx(
-                out=codes[:].bitcast(FP8X4),
-                scales=scales[:],
-                in_=grouped[:].rearrange("p c a d t -> p (c a d t)"),
-            )
 
         k_grouped_tiles = []
         q_grouped_tiles = []
@@ -90,18 +84,26 @@ def tile_flaxattention2_s_kernel(tc, query, key, value, out):
         def quantise_k(pair):
             k_codes = operands.tile([P, PASSES * COLS], U32, align_bytes=64)
             k_scales = operands.tile([P, PASSES * COLS], U8, align_bytes=64)
-            quantise(k_grouped_tiles[pair], k_codes, k_scales)
+            nc.vector.quantize_mx(
+                out=k_codes[:].bitcast(FP8X4),
+                scales=k_scales[:],
+                in_=k_grouped_tiles[pair][:].rearrange("p c a d t -> p (c a d t)"),
+            )
             k_code_tiles.append(k_codes)
             k_scale_tiles.append(k_scales)
 
         def quantise_q_and_multiply(pair):
             q_codes = operands.tile([P, PASSES * COLS], U32, align_bytes=64)
             q_scales = operands.tile([P, PASSES * COLS], U8, align_bytes=64)
-            quantise(q_grouped_tiles[pair], q_codes, q_scales)
             scores = psum.tile([P, COLS], F32)
             score_tiles.append(scores)
             for c in range(PASSES):
                 cols = slice(c * COLS, (c + 1) * COLS)
+                nc.vector.quantize_mx(
+                    out=q_codes[:, cols].bitcast(FP8X4),
+                    scales=q_scales[:, cols],
+                    in_=q_grouped_tiles[pair][:, c].rearrange("p a d t -> p (a d t)"),
+                )
                 nc.tensor.matmul_mx(
                     out=scores[:],
                     lhsT=q_codes[:, cols].bitcast(FP8X4),

@@ -39,7 +39,6 @@ def tile_flaxattention2_s_kernel(tc, query, key, value, out):
     out_view = out.rearrange("(pair a) d e -> (a d) pair e", a=DUO)
 
     with ExitStack() as ctx:
-        ctx.enter_context(tc.manual_schedule())
         loads = ctx.enter_context(tc.tile_pool(name="loads", bufs=PAIRS))
         operands = ctx.enter_context(tc.tile_pool(name="operands", bufs=PAIRS))
         soft = ctx.enter_context(tc.tile_pool(name="soft", bufs=1))
@@ -64,6 +63,12 @@ def tile_flaxattention2_s_kernel(tc, query, key, value, out):
             regroup(nc.scalar.copy, raw[:, :, 0], grouped[:, 0])
             regroup(nc.vector.tensor_copy, raw[:, :, 1], grouped[:, 1])
 
+        def quantise(grouped, codes, scales):
+            nc.vector.quantize_mx(
+                out=codes[:].bitcast(FP8X4),
+                scales=scales[:],
+                in_=grouped[:].rearrange("p c a d t -> p (c a d t)"),
+            )
 
         k_grouped_tiles = []
         q_grouped_tiles = []
@@ -84,26 +89,18 @@ def tile_flaxattention2_s_kernel(tc, query, key, value, out):
         def quantise_k(pair):
             k_codes = operands.tile([P, PASSES * COLS], U32, align_bytes=64)
             k_scales = operands.tile([P, PASSES * COLS], U8, align_bytes=64)
-            nc.vector.quantize_mx(
-                out=k_codes[:].bitcast(FP8X4),
-                scales=k_scales[:],
-                in_=k_grouped_tiles[pair][:].rearrange("p c a d t -> p (c a d t)"),
-            )
+            quantise(k_grouped_tiles[pair], k_codes, k_scales)
             k_code_tiles.append(k_codes)
             k_scale_tiles.append(k_scales)
 
         def quantise_q_and_multiply(pair):
             q_codes = operands.tile([P, PASSES * COLS], U32, align_bytes=64)
             q_scales = operands.tile([P, PASSES * COLS], U8, align_bytes=64)
+            quantise(q_grouped_tiles[pair], q_codes, q_scales)
             scores = psum.tile([P, COLS], F32)
             score_tiles.append(scores)
             for c in range(PASSES):
                 cols = slice(c * COLS, (c + 1) * COLS)
-                nc.vector.quantize_mx(
-                    out=q_codes[:, cols].bitcast(FP8X4),
-                    scales=q_scales[:, cols],
-                    in_=q_grouped_tiles[pair][:, c].rearrange("p a d t -> p (a d t)"),
-                )
                 nc.tensor.matmul_mx(
                     out=scores[:],
                     lhsT=q_codes[:, cols].bitcast(FP8X4),

from contextlib import ExitStack

import concourse.mybir as mybir

BF16 = mybir.dt.bfloat16
F32 = mybir.dt.float32
U32 = mybir.dt.uint32
U8 = mybir.dt.uint8
FP8X4 = mybir.dt.float8_e4m3fn_x4
ALU = mybir.AluOpType
ACT = mybir.ActivationFunctionType

P = 128
PACK = 4
SEQ, HEADS, DH = 1024, 8, 64
MATS = SEQ // P
PASSES = HEADS // PACK
DUO = 2
PAIRS = MATS // DUO
COLS = DUO * DH
RUN = 4
SCALE = DH ** -0.5

FLOPS = 2 * MATS * DH * DH * SEQ
BYTES = 2 * SEQ * HEADS * DH * 2 + MATS * DH * DH * 4


def regroup(copy, raw, grouped):
    copy(
        out=grouped.rearrange("p a (e i) t -> p a e t i", i=RUN),
        in_=raw.rearrange("p a t (e i) -> p a e t i", i=RUN),
    )


def tile_flaxattention2_s_kernel(tc, query, key, value, out):
    nc = tc.nc
    q_view = query.rearrange("b (j g) (c t) d -> (b j) g c t d", g=MATS, t=PACK)
    k_view = key.rearrange("b (j g) (c t) d -> (b j) g c t d", g=MATS, t=PACK)
    out_view = out.rearrange("(pair a) d e -> (a d) pair e", a=DUO)

    with ExitStack() as ctx:
        loads = ctx.enter_context(tc.tile_pool(name="loads", bufs=PAIRS))
        operands = ctx.enter_context(tc.tile_pool(name="operands", bufs=PAIRS))
        soft = ctx.enter_context(tc.tile_pool(name="soft", bufs=1))
        psum = ctx.enter_context(tc.psum_pool(name="psum", bufs=PAIRS))

        k_raw_tiles = []
        q_raw_tiles = []
        for pair in range(PAIRS):
            mats = slice(pair * DUO, (pair + 1) * DUO)
            k_raw = loads.tile([P, DUO, PASSES, PACK, DH], BF16)
            nc.sync.dma_start(out=k_raw[:], in_=k_view[:, mats])
            k_raw_tiles.append(k_raw)
            q_raw = loads.tile([P, DUO, PASSES, PACK, DH], BF16)
            nc.sync.dma_start(out=q_raw[:], in_=q_view[:, mats])
            q_raw_tiles.append(q_raw)

        warm = soft.tile([P, 1], F32)
        nc.vector.memset(warm[:], 0.0)
        nc.scalar.activation(out=warm[:], in_=warm[:], func=ACT.Exp)

        def regroup_both_passes(raw, grouped):
            regroup(nc.scalar.copy, raw[:, :, 0], grouped[:, 0])
            regroup(nc.vector.tensor_copy, raw[:, :, 1], grouped[:, 1])

        def quantise(grouped, codes, scales):
            nc.vector.quantize_mx(
                out=codes[:].bitcast(FP8X4),
                scales=scales[:],
                in_=grouped[:].rearrange("p c a d t -> p (c a d t)"),
            )

        k_grouped_tiles = []
        q_grouped_tiles = []
        k_code_tiles = []
        k_scale_tiles = []
        score_tiles = []

        def regroup_k(pair):
            k_grouped = operands.tile([P, PASSES, DUO, DH, PACK], BF16, align_bytes=64)
            regroup_both_passes(k_raw_tiles[pair], k_grouped)
            k_grouped_tiles.append(k_grouped)

        def regroup_q(pair):
            q_grouped = operands.tile([P, PASSES, DUO, DH, PACK], BF16, align_bytes=64)
            regroup_both_passes(q_raw_tiles[pair], q_grouped)
            q_grouped_tiles.append(q_grouped)

        def quantise_k(pair):
            k_codes = operands.tile([P, PASSES * COLS], U32, align_bytes=64)
            k_scales = operands.tile([P, PASSES * COLS], U8, align_bytes=64)
            quantise(k_grouped_tiles[pair], k_codes, k_scales)
            k_code_tiles.append(k_codes)
            k_scale_tiles.append(k_scales)

        def quantise_q_and_multiply(pair):
            q_codes = operands.tile([P, PASSES * COLS], U32, align_bytes=64)
            q_scales = operands.tile([P, PASSES * COLS], U8, align_bytes=64)
            quantise(q_grouped_tiles[pair], q_codes, q_scales)
            scores = psum.tile([P, COLS], F32)
            score_tiles.append(scores)
            for c in range(PASSES):
                cols = slice(c * COLS, (c + 1) * COLS)
                nc.tensor.matmul_mx(
                    out=scores[:],
                    lhsT=q_codes[:, cols].bitcast(FP8X4),
                    lhsT_scale=q_scales[:, cols],
                    rhs=k_code_tiles[pair][:, cols].bitcast(FP8X4),
                    rhs_scale=k_scale_tiles[pair][:, cols],
                    start=(c == 0),
                    stop=(c == PASSES - 1),
                )

        for pair in range(PAIRS):
            regroup_k(pair)
            if pair > 0:
                quantise_q_and_multiply(pair - 1)
            regroup_q(pair)
            quantise_k(pair)
        quantise_q_and_multiply(PAIRS - 1)

        flipped = soft.tile([P, PAIRS, DH], F32)
        shift = soft.tile([P, PAIRS], F32)
        grown = soft.tile([P, PAIRS, DH], F32)
        row_sum = soft.tile([P, PAIRS], F32)
        inverse = soft.tile([P, PAIRS], F32)
        probs = soft.tile([P, PAIRS, DH], F32)

        for pair in range(PAIRS):
            one = slice(pair, pair + 1)
            for a in range(DUO):
                half = slice(a * DH, (a + 1) * DH)
                nc.vector.tensor_scalar(
                    out=flipped[half, pair, :],
                    in0=score_tiles[pair][half, half],
                    scalar1=-SCALE,
                    scalar2=None,
                    op0=ALU.mult,
                    op1=ALU.min,
                    accum_out=shift[half, one],
                )
            nc.scalar.activation(
                out=grown[:, pair, :],
                in_=flipped[:, pair, :],
                func=ACT.Exp,
                bias=shift[:, one],
                scale=-1.0,
                accum_out=row_sum[:, one],
            )

        for group in (range(PAIRS - 1), range(PAIRS - 1, PAIRS)):
            for pair in group:
                one = slice(pair, pair + 1)
                nc.vector.reciprocal(out=inverse[:, one], in_=row_sum[:, one])
            for pair in group:
                one = slice(pair, pair + 1)
                nc.vector.tensor_scalar(
                    out=probs[:, pair, :],
                    in0=grown[:, pair, :],
                    scalar1=inverse[:, one],
                    scalar2=None,
                    op0=ALU.mult,
                )
                nc.sync.dma_start(out=out_view[:, pair, :], in_=probs[:, pair, :])
